import numpy as np
import ml_dtypes


def mxq(x, axis, fmt="e4m3"):
    dtype, down = {"e4m3": (ml_dtypes.float8_e4m3fn, 7), "e5m2": (ml_dtypes.float8_e5m2, 14)}[fmt]
    v = np.moveaxis(np.asarray(x, np.float32).astype(ml_dtypes.bfloat16).astype(np.float64), axis, -1)
    blocks = v.reshape(v.shape[:-1] + (-1, 32))
    amax = np.abs(blocks).max(-1, keepdims=True)
    byte = np.maximum(np.where(amax > 0, np.frexp(amax)[1] - 1 + 127, 0) - down, 1)
    scale = np.exp2(byte - 127.0)
    codes = (blocks / scale).astype(np.float32).astype(dtype).astype(np.float64)
    return np.moveaxis((codes * scale).reshape(v.shape), -1, axis)


WIDE = False


def mx_kscale(k):
    if not WIDE:
        return np.ones(k)
    levels = np.array([10, -10, 5, -5, 0])
    a = np.random.permutation(np.resize(levels, k // 512 * 4)).reshape(k // 512, 4)
    idx = np.arange(k)
    return np.exp2(a[idx // 512, idx % 128 // 32])


BF16 = ml_dtypes.bfloat16


def bf(x):
    return np.asarray(x, np.float32).astype(BF16)


def f64(x):
    return np.asarray(x).astype(np.float64)


B, N, C, H = 4, 1024, 512, 1024
EPS = 1e-12


def layer_norm(v, w, b):
    u = v.mean(-1, keepdims=True)
    s = ((v - u) ** 2).mean(-1, keepdims=True)
    return w * ((v - u) / np.sqrt(s + EPS)) + b


def setup_inputs():
    s = mx_kscale(C)
    x = np.random.standard_normal((B, N, C)) * (0.4 + 1.2 * np.random.random((B, N)))[:, :, None] + 0.4 * np.random.standard_normal((B, N))[:, :, None]
    return {"x": bf(x),
            "pre_w": bf((1.0 + 0.1 * np.random.standard_normal(C)) * s),
            "pre_b": bf(0.2 * np.random.standard_normal(C) * s),
            "lin1_W": bf(np.random.standard_normal((H, C)) / np.sqrt(C) / s[None, :]),
            "lin1_b": bf(0.3 * np.random.standard_normal(H) + 0.3),
            "n1_w": bf(1.0 + 0.1 * np.random.standard_normal(H)),
            "n1_b": bf(0.2 * np.random.standard_normal(H))}


def reference(x, pre_w, pre_b, lin1_W, lin1_b, n1_w, n1_b):
    y = np.maximum(layer_norm(f64(x), f64(pre_w), f64(pre_b)), 0.0)
    y = (mxq(y, 2, "e4m3") @ mxq(f64(lin1_W), 1, "e4m3").T) + f64(lin1_b)
    return np.maximum(layer_norm(y, f64(n1_w), f64(n1_b)), 0.0)

@@ -1,0 +1,227 @@
+from contextlib import ExitStack
+
+import concourse.mybir as mybir
+from concourse.masks import make_identity
+
+F32 = mybir.dt.float32
+BF16 = mybir.dt.bfloat16
+U32 = mybir.dt.uint32
+U8 = mybir.dt.uint8
+FP8X4 = mybir.dt.float8_e4m3fn_x4
+ALU = mybir.AluOpType
+ACT = mybir.ActivationFunctionType
+AXIS = mybir.AxisListType
+
+P = 128
+PACK = 4
+ROWS = 4 * 1024
+C = 512
+H = 1024
+EPS = 1e-12
+ROW_TILES = 4
+BLOCK = ROW_TILES * P
+BLOCKS = ROWS // BLOCK
+BANK = 512
+HALVES = H // BANK
+H_TILES = H // P
+BN_STATS_DIM = 6
+BN_AGGR_DIM = 2
+PRE_W, PRE_B, N1_W, N1_B = 0, PACK, 2 * PACK, 2 * PACK + H_TILES
+PARAM_COLS = 2 * PACK + 2 * H_TILES
+
+FLOPS = 2 * ROWS * C * H
+
+
+def tile_graphresblock_pa_t_kernel(tc, x, pre_w, pre_b, lin1_W, lin1_b, n1_w, n1_b, out):
+    nc = tc.nc
+    x_blocks = x.flatten_outer_dims().rearrange("(b p i) c -> b p i c", p=P, i=ROW_TILES)
+    out_blocks = out.flatten_outer_dims().rearrange("(b p i) h -> b p i h", p=P, i=ROW_TILES)
+
+    with ExitStack() as ctx:
+        keep = ctx.enter_context(tc.tile_pool(name="keep", bufs=1))
+        small = ctx.enter_context(tc.tile_pool(name="small", bufs=3))
+        work = ctx.enter_context(tc.tile_pool(name="work", bufs=2))
+        psum = ctx.enter_context(tc.psum_pool(name="psum", bufs=2))
+
+        ident_f32 = keep.tile([P, P], F32)
+        make_identity(nc, ident_f32[:])
+        ident_bf16 = keep.tile([P, P], BF16)
+        make_identity(nc, ident_bf16[:])
+        eps = keep.tile([P, 1], F32)
+        nc.vector.memset(eps[:], EPS)
+
+        param_rows = keep.tile([P, P], BF16)
+        nc.vector.memset(param_rows[:], 0.0)
+        for first, vector in ((PRE_W, pre_w), (PRE_B, pre_b), (N1_W, n1_w), (N1_B, n1_b)):
+            rows = vector.rearrange("(t p) -> t p", p=P)
+            nc.sync.dma_start(out=param_rows[first : first + rows.shape[0], :], in_=rows)
+
+        x_all = keep.tile([P, BLOCKS, ROW_TILES, C], BF16)
+        nc.sync.dma_start(out=x_all[:, 0], in_=x_blocks[0])
+        w_rows = keep.tile([P, H_TILES, C], BF16)
+        nc.sync.dma_start(out=w_rows[:], in_=lin1_W.rearrange("(j p) c -> p j c", p=P))
+        for b in range(1, BLOCKS):
+            nc.sync.dma_start(out=x_all[:, b], in_=x_blocks[b])
+        bias_all = keep.tile([P, H], BF16)
+        nc.sync.dma_start(out=bias_all[:], in_=lin1_b.partition_broadcast(P))
+
+        params_ps = psum.tile([P, P], BF16, tag="channels1")
+        nc.tensor.transpose(params_ps[:], param_rows[:], ident_bf16[:])
+        params = keep.tile([P, PARAM_COLS], F32)
+        nc.vector.tensor_copy(out=params[:], in_=params_ps[:, 0:PARAM_COLS])
+
+        w_grouped = keep.tile([P, H, PACK], BF16, align_bytes=64)
+        for j in range(H_TILES):
+            w_ps = psum.tile([P, PACK, P], BF16, tag="channels1")
+            for t in range(PACK):
+                nc.tensor.transpose(w_ps[:, t, :], w_rows[:, j, t * P : (t + 1) * P], ident_bf16[:])
+            nc.vector.tensor_copy(
+                out=w_grouped[:, j * P : (j + 1) * P, :], in_=w_ps[:].rearrange("p t h -> p h t")
+            )
+        w_codes = keep.tile([P, H], U32, align_bytes=64)
+        w_scales = keep.tile([P, H], U8, align_bytes=64)
+        nc.vector.quantize_mx(
+            out=w_codes[:].bitcast(FP8X4),
+            scales=w_scales[:],
+            in_=w_grouped[:].rearrange("p h t -> p (h t)"),
+        )
+
+        def first_norm(b):
+            stats = small.tile([P, ROW_TILES, BN_STATS_DIM], F32, name="stats")
+            mean_var = small.tile([P, ROW_TILES, BN_AGGR_DIM], F32, name="mean_var")
+            for i in range(ROW_TILES):
+                nc.vector.bn_stats(out=stats[:, i, :], in_=x_all[:, b, i, :])
+            for i in range(ROW_TILES):
+                nc.vector.bn_aggr(out=mean_var[:, i, :], in_=stats[:, i, :])
+            std = small.tile([P, ROW_TILES], F32, name="std1")
+            nc.scalar.activation(out=std[:], in_=mean_var[:, :, 1], func=ACT.Sqrt, bias=eps[:, 0:1], scale=1.0)
+            rstd = small.tile([P, ROW_TILES], F32, name="rstd1")
+            nc.vector.reciprocal(out=rstd[:], in_=std[:])
+            neg_mean = small.tile([P, ROW_TILES], F32, name="neg_mean1")
+            nc.vector.tensor_scalar_mul(out=neg_mean[:], in0=mean_var[:, :, 0], scalar1=-1.0)
+
+            normed = work.tile([P, ROW_TILES, C], F32, name="normed1")
+            for i in range(ROW_TILES):
+                nc.gpsimd.tensor_scalar(
+                    out=normed[:, i, :],
+                    in0=x_all[:, b, i, :],
+                    scalar1=neg_mean[:, i : i + 1],
+                    scalar2=rstd[:, i : i + 1],
+                    op0=ALU.add,
+                    op1=ALU.mult,
+                )
+
+            y0T = work.tile([P, PACK, BLOCK], BF16, name="y0T")
+            for t in range(PACK):
+                channels = psum.tile([P, BLOCK], F32, tag="channels1")
+                for i in range(ROW_TILES):
+                    nc.tensor.transpose(
+                        channels[:, i * P : (i + 1) * P], normed[:, i, t * P : (t + 1) * P], ident_f32[:]
+                    )
+                nc.scalar.activation(
+                    out=y0T[:, t, :],
+                    in_=channels[:],
+                    func=ACT.Relu,
+                    bias=params[:, PRE_B + t : PRE_B + t + 1],
+                    scale=params[:, PRE_W + t : PRE_W + t + 1],
+                )
+            grouped = work.tile([P, BLOCK, PACK], BF16, name="grouped", align_bytes=64)
+            nc.vector.tensor_copy(out=grouped[:], in_=y0T[:].rearrange("p t n -> p n t"))
+            codes = work.tile([P, BLOCK], U32, name="codes", align_bytes=64)
+            scales = work.tile([P, BLOCK], U8, name="scales", align_bytes=64)
+            nc.vector.quantize_mx(
+                out=codes[:].bitcast(FP8X4), scales=scales[:], in_=grouped[:].rearrange("p n t -> p (n t)")
+            )
+            return codes, scales
+
+        def project_and_norm(b, codes, scales):
+            y1 = work.tile([P, ROW_TILES, H], F32, name="y1")
+            row_sums = small.tile([P, ROW_TILES, HALVES], F32, name="row_sums")
+            for i in range(ROW_TILES):
+                rows = slice(i * P, (i + 1) * P)
+                for half in range(HALVES):
+                    cols = slice(half * BANK, (half + 1) * BANK)
+                    acc = psum.tile([P, BANK], F32, tag="acc")
+                    nc.tensor.matmul_mx(
+                        out=acc[:],
+                        lhsT=codes[:, rows].bitcast(FP8X4),
+                        lhsT_scale=scales[:, rows],
+                        rhs=w_codes[:, cols].bitcast(FP8X4),
+                        rhs_scale=w_scales[:, cols],
+                        start=True,
+                        stop=True,
+                    )
+                    nc.vector.scalar_tensor_tensor(
+                        out=y1[:, i, cols],
+                        in0=acc[:],
+                        scalar=0.0,
+                        in1=bias_all[:, cols],
+                        op0=ALU.add,
+                        op1=ALU.add,
+                        accum_out=row_sums[:, i, half : half + 1],
+                    )
+            total = small.tile([P, ROW_TILES], F32, name="total")
+            nc.vector.tensor_reduce(out=total[:], in_=row_sums[:], axis=AXIS.X, op=ALU.add)
+            neg_mean = small.tile([P, ROW_TILES], F32, name="neg_mean2")
+            nc.vector.tensor_scalar_mul(out=neg_mean[:], in0=total[:], scalar1=-1.0 / H)
+
+            squares = small.tile([P, ROW_TILES], F32, name="squares")
+            for i in range(ROW_TILES):
+                unread = work.tile([P, H], BF16, name="unread")
+                nc.scalar.activation(
+                    out=unread[:],
+                    in_=y1[:, i, :],
+                    func=ACT.Square,
+                    bias=neg_mean[:, i : i + 1],
+                    scale=1.0,
+                    accum_out=squares[:, i : i + 1],
+                )
+            std = small.tile([P, ROW_TILES], F32, name="std2")
+            nc.scalar.activation(out=std[:], in_=squares[:], func=ACT.Sqrt, bias=eps[:, 0:1], scale=1.0 / H)
+            rstd = small.tile([P, ROW_TILES], F32, name="rstd2")
+            nc.vector.reciprocal(out=rstd[:], in_=std[:])
+            for i in range(ROW_TILES):
+                nc.gpsimd.tensor_scalar(
+                    out=y1[:, i, :],
+                    in0=y1[:, i, :],
+                    scalar1=neg_mean[:, i : i + 1],
+                    scalar2=rstd[:, i : i + 1],
+                    op0=ALU.add,
+                    op1=ALU.mult,
+                )
+            return y1
+
+        def gain_bias_relu_store(b, normed):
+            resultT = work.tile([P, H_TILES, BLOCK], F32, name="resultT")
+            for j in range(H_TILES):
+                features = psum.tile([P, BLOCK], F32, tag="features")
+                for i in range(ROW_TILES):
+                    nc.tensor.transpose(
+                        features[:, i * P : (i + 1) * P], normed[:, i, j * P : (j + 1) * P], ident_f32[:]
+                    )
+                nc.scalar.activation(
+                    out=resultT[:, j, :],
+                    in_=features[:],
+                    func=ACT.Relu,
+                    bias=params[:, N1_B + j : N1_B + j + 1],
+                    scale=params[:, N1_W + j : N1_W + j + 1],
+                )
+            result = work.tile([P, ROW_TILES, H], F32, name="result")
+            for i in range(ROW_TILES):
+                for half in range(HALVES):
+                    back = psum.tile([P, BANK], F32, tag="back")
+                    for q in range(BANK // P):
+                        j = half * (BANK // P) + q
+                        nc.tensor.transpose(
+                            back[:, q * P : (q + 1) * P], resultT[:, j, i * P : (i + 1) * P], ident_f32[:]
+                        )
+                    if i == ROW_TILES - 1:
+                        nc.scalar.copy(out=result[:, i, half * BANK : (half + 1) * BANK], in_=back[:])
+                    else:
+                        nc.vector.tensor_copy(out=result[:, i, half * BANK : (half + 1) * BANK], in_=back[:])
+                nc.sync.dma_start(out=out_blocks[b][:, i, :], in_=result[:, i, :])
+
+        for b in range(BLOCKS):
+            codes, scales = first_norm(b)
+            normed = project_and_norm(b, codes, scales)
+            gain_bias_relu_store(b, normed)

@@ -18,210 +18,302 @@ ROWS = 4 * 1024
 C = 512
 H = 1024
 EPS = 1e-12
-ROW_TILES = 4
-BLOCK = ROW_TILES * P
+QUARTERS = 4
+BLOCK = QUARTERS * P
 BLOCKS = ROWS // BLOCK
 BANK = 512
 HALVES = H // BANK
 H_TILES = H // P
+TILES_PER_BANK = BANK // P
+TILES_PER_STEP = H_TILES // QUARTERS
 BN_STATS_DIM = 6
 BN_AGGR_DIM = 2
 PRE_W, PRE_B, N1_W, N1_B = 0, PACK, 2 * PACK, 2 * PACK + H_TILES
 PARAM_COLS = 2 * PACK + 2 * H_TILES
 
+LAG_STATS = 0
+LAG_SCALARS1 = LAG_STATS + QUARTERS - 1
+LAG_NORM1 = LAG_STATS + QUARTERS
+LAG_WEIGHTS = LAG_NORM1
+LAG_CHANNELS = LAG_NORM1 + QUARTERS
+LAG_QUANTISE = LAG_CHANNELS + QUARTERS
+LAG_PROJECT = LAG_QUANTISE + 1
+LAG_MEAN2 = LAG_PROJECT + QUARTERS - 1
+LAG_SQUARES = LAG_PROJECT + QUARTERS
+LAG_RSTD2 = LAG_SQUARES + QUARTERS - 1
+LAG_NORM2 = LAG_SQUARES + QUARTERS
+LAG_FEATURES = LAG_NORM2 + QUARTERS
+LAG_BACK = LAG_FEATURES + QUARTERS // HALVES
+STEPS = LAG_BACK + BLOCKS * QUARTERS
+
 FLOPS = 2 * ROWS * C * H
+
+
+def quarter_of(step, lag):
+    index = step - lag
+    if 0 <= index < BLOCKS * QUARTERS:
+        return divmod(index, QUARTERS)
+    return None
+
+
+def block_of(step, lag):
+    index = step - lag
+    if index >= 0 and index % QUARTERS == 0 and index // QUARTERS < BLOCKS:
+        return index // QUARTERS
+    return None
 
 
 def tile_graphresblock_pa_t_kernel(tc, x, pre_w, pre_b, lin1_W, lin1_b, n1_w, n1_b, out):
     nc = tc.nc
-    x_blocks = x.flatten_outer_dims().rearrange("(b p i) c -> b p i c", p=P, i=ROW_TILES)
-    out_blocks = out.flatten_outer_dims().rearrange("(b p i) h -> b p i h", p=P, i=ROW_TILES)
+    x_blocks = x.flatten_outer_dims().rearrange("(b p i) c -> b p i c", p=P, i=QUARTERS)
+    out_blocks = out.flatten_outer_dims().rearrange("(b p i) h -> b p i h", p=P, i=QUARTERS)
 
     with ExitStack() as ctx:
+        ctx.enter_context(tc.manual_schedule())
         keep = ctx.enter_context(tc.tile_pool(name="keep", bufs=1))
-        small = ctx.enter_context(tc.tile_pool(name="small", bufs=3))
+        small = ctx.enter_context(tc.tile_pool(name="small", bufs=4))
         work = ctx.enter_context(tc.tile_pool(name="work", bufs=2))
         psum = ctx.enter_context(tc.psum_pool(name="psum", bufs=2))
 
-        ident_f32 = keep.tile([P, P], F32)
-        make_identity(nc, ident_f32[:])
-        ident_bf16 = keep.tile([P, P], BF16)
-        make_identity(nc, ident_bf16[:])
         eps = keep.tile([P, 1], F32)
         nc.vector.memset(eps[:], EPS)
-
+        table_warmer = keep.tile([P, 1], F32)
+        nc.scalar.activation(out=table_warmer[:], in_=eps[:], func=ACT.Abs_reciprocal_sqrt)
         param_rows = keep.tile([P, P], BF16)
         nc.vector.memset(param_rows[:], 0.0)
+        ident_bf16 = keep.tile([P, P], BF16)
+        make_identity(nc, ident_bf16[:])
+        ident_f32 = keep.tile([P, P], F32)
+        make_identity(nc, ident_f32[:])
+
+        x_tiles = [keep.tile([P, QUARTERS, C], BF16, name="x%d" % b) for b in range(BLOCKS)]
+        w_rows = keep.tile([P, H_TILES, C], BF16)
+        bias_all = keep.tile([P, H], BF16)
+        nc.sync.dma_start(out=x_tiles[0][:], in_=x_blocks[0])
         for first, vector in ((PRE_W, pre_w), (PRE_B, pre_b), (N1_W, n1_w), (N1_B, n1_b)):
             rows = vector.rearrange("(t p) -> t p", p=P)
             nc.sync.dma_start(out=param_rows[first : first + rows.shape[0], :], in_=rows)
-
-        x_all = keep.tile([P, BLOCKS, ROW_TILES, C], BF16)
-        nc.sync.dma_start(out=x_all[:, 0], in_=x_blocks[0])
-        w_rows = keep.tile([P, H_TILES, C], BF16)
+        nc.sync.dma_start(out=x_tiles[1][:], in_=x_blocks[1])
         nc.sync.dma_start(out=w_rows[:], in_=lin1_W.rearrange("(j p) c -> p j c", p=P))
-        for b in range(1, BLOCKS):
-            nc.sync.dma_start(out=x_all[:, b], in_=x_blocks[b])
-        bias_all = keep.tile([P, H], BF16)
+        for b in range(2, BLOCKS):
+            nc.sync.dma_start(out=x_tiles[b][:], in_=x_blocks[b])
         nc.sync.dma_start(out=bias_all[:], in_=lin1_b.partition_broadcast(P))
 
-        params_ps = psum.tile([P, P], BF16, tag="channels1")
+        params_ps = psum.tile([P, P], BF16, tag="channels")
         nc.tensor.transpose(params_ps[:], param_rows[:], ident_bf16[:])
         params = keep.tile([P, PARAM_COLS], F32)
-        nc.vector.tensor_copy(out=params[:], in_=params_ps[:, 0:PARAM_COLS])
+        nc.scalar.copy(out=params[:], in_=params_ps[:, 0:PARAM_COLS])
 
         w_grouped = keep.tile([P, H, PACK], BF16, align_bytes=64)
-        for j in range(H_TILES):
-            w_ps = psum.tile([P, PACK, P], BF16, tag="channels1")
-            for t in range(PACK):
-                nc.tensor.transpose(w_ps[:, t, :], w_rows[:, j, t * P : (t + 1) * P], ident_bf16[:])
-            nc.vector.tensor_copy(
-                out=w_grouped[:, j * P : (j + 1) * P, :], in_=w_ps[:].rearrange("p t h -> p h t")
-            )
         w_codes = keep.tile([P, H], U32, align_bytes=64)
         w_scales = keep.tile([P, H], U8, align_bytes=64)
-        nc.vector.quantize_mx(
-            out=w_codes[:].bitcast(FP8X4),
-            scales=w_scales[:],
-            in_=w_grouped[:].rearrange("p h t -> p (h t)"),
-        )
 
-        def first_norm(b):
-            stats = small.tile([P, ROW_TILES, BN_STATS_DIM], F32, name="stats")
-            mean_var = small.tile([P, ROW_TILES, BN_AGGR_DIM], F32, name="mean_var")
-            for i in range(ROW_TILES):
-                nc.vector.bn_stats(out=stats[:, i, :], in_=x_all[:, b, i, :])
-            for i in range(ROW_TILES):
-                nc.vector.bn_aggr(out=mean_var[:, i, :], in_=stats[:, i, :])
-            std = small.tile([P, ROW_TILES], F32, name="std1")
-            nc.scalar.activation(out=std[:], in_=mean_var[:, :, 1], func=ACT.Sqrt, bias=eps[:, 0:1], scale=1.0)
-            rstd = small.tile([P, ROW_TILES], F32, name="rstd1")
-            nc.vector.reciprocal(out=rstd[:], in_=std[:])
-            neg_mean = small.tile([P, ROW_TILES], F32, name="neg_mean1")
-            nc.vector.tensor_scalar_mul(out=neg_mean[:], in0=mean_var[:, :, 0], scalar1=-1.0)
-
-            normed = work.tile([P, ROW_TILES, C], F32, name="normed1")
-            for i in range(ROW_TILES):
-                nc.gpsimd.tensor_scalar(
-                    out=normed[:, i, :],
-                    in0=x_all[:, b, i, :],
-                    scalar1=neg_mean[:, i : i + 1],
-                    scalar2=rstd[:, i : i + 1],
-                    op0=ALU.add,
-                    op1=ALU.mult,
-                )
-
-            y0T = work.tile([P, PACK, BLOCK], BF16, name="y0T")
+        def turn_weights(j):
+            w_ps = psum.tile([P, PACK, P], BF16, tag="channels")
             for t in range(PACK):
-                channels = psum.tile([P, BLOCK], F32, tag="channels1")
-                for i in range(ROW_TILES):
-                    nc.tensor.transpose(
-                        channels[:, i * P : (i + 1) * P], normed[:, i, t * P : (t + 1) * P], ident_f32[:]
-                    )
-                nc.scalar.activation(
-                    out=y0T[:, t, :],
-                    in_=channels[:],
-                    func=ACT.Relu,
-                    bias=params[:, PRE_B + t : PRE_B + t + 1],
-                    scale=params[:, PRE_W + t : PRE_W + t + 1],
-                )
-            grouped = work.tile([P, BLOCK, PACK], BF16, name="grouped", align_bytes=64)
-            nc.vector.tensor_copy(out=grouped[:], in_=y0T[:].rearrange("p t n -> p n t"))
-            codes = work.tile([P, BLOCK], U32, name="codes", align_bytes=64)
-            scales = work.tile([P, BLOCK], U8, name="scales", align_bytes=64)
+                nc.tensor.transpose(w_ps[:, t, :], w_rows[:, j, t * P : (t + 1) * P], ident_bf16[:])
+            nc.scalar.copy(out=w_grouped[:, j * P : (j + 1) * P, :], in_=w_ps[:].rearrange("p t h -> p h t"))
+
+        def quantise_weights():
             nc.vector.quantize_mx(
-                out=codes[:].bitcast(FP8X4), scales=scales[:], in_=grouped[:].rearrange("p n t -> p (n t)")
+                out=w_codes[:].bitcast(FP8X4),
+                scales=w_scales[:],
+                in_=w_grouped[:].rearrange("p h t -> p (h t)"),
             )
-            return codes, scales
 
-        def project_and_norm(b, codes, scales):
-            y1 = work.tile([P, ROW_TILES, H], F32, name="y1")
-            row_sums = small.tile([P, ROW_TILES, HALVES], F32, name="row_sums")
-            for i in range(ROW_TILES):
-                rows = slice(i * P, (i + 1) * P)
-                for half in range(HALVES):
-                    cols = slice(half * BANK, (half + 1) * BANK)
-                    acc = psum.tile([P, BANK], F32, tag="acc")
-                    nc.tensor.matmul_mx(
-                        out=acc[:],
-                        lhsT=codes[:, rows].bitcast(FP8X4),
-                        lhsT_scale=scales[:, rows],
-                        rhs=w_codes[:, cols].bitcast(FP8X4),
-                        rhs_scale=w_scales[:, cols],
-                        start=True,
-                        stop=True,
-                    )
-                    nc.vector.scalar_tensor_tensor(
-                        out=y1[:, i, cols],
-                        in0=acc[:],
-                        scalar=0.0,
-                        in1=bias_all[:, cols],
-                        op0=ALU.add,
-                        op1=ALU.add,
-                        accum_out=row_sums[:, i, half : half + 1],
-                    )
-            total = small.tile([P, ROW_TILES], F32, name="total")
-            nc.vector.tensor_reduce(out=total[:], in_=row_sums[:], axis=AXIS.X, op=ALU.add)
-            neg_mean = small.tile([P, ROW_TILES], F32, name="neg_mean2")
-            nc.vector.tensor_scalar_mul(out=neg_mean[:], in0=total[:], scalar1=-1.0 / H)
+        stats, neg_mean1, rstd1, normed1, y0T, grouped, codes, scales = {}, {}, {}, {}, {}, {}, {}, {}
+        y1, row_sums, neg_mean2, squares, rstd2, resultT = {}, {}, {}, {}, {}, {}
 
-            squares = small.tile([P, ROW_TILES], F32, name="squares")
-            for i in range(ROW_TILES):
-                unread = work.tile([P, H], BF16, name="unread")
-                nc.scalar.activation(
-                    out=unread[:],
-                    in_=y1[:, i, :],
-                    func=ACT.Square,
-                    bias=neg_mean[:, i : i + 1],
-                    scale=1.0,
-                    accum_out=squares[:, i : i + 1],
+        def stats_of_x(b, i):
+            if i == 0:
+                stats[b] = small.tile([P, QUARTERS, BN_STATS_DIM], F32, name="stats")
+            nc.vector.bn_stats(out=stats[b][:, i, :], in_=x_tiles[b][:, i, :])
+
+        def scalars_of_x(b):
+            mean_var = small.tile([P, QUARTERS, BN_AGGR_DIM], F32, name="mean_var")
+            for i in range(QUARTERS):
+                nc.vector.bn_aggr(out=mean_var[:, i, :], in_=stats[b][:, i, :])
+            neg_mean1[b] = small.tile([P, QUARTERS], F32, name="neg_mean1")
+            nc.vector.tensor_scalar_mul(out=neg_mean1[b][:], in0=mean_var[:, :, 0], scalar1=-1.0)
+            rstd1[b] = small.tile([P, QUARTERS], F32, name="rstd1")
+            nc.scalar.activation(
+                out=rstd1[b][:], in_=mean_var[:, :, 1], func=ACT.Abs_reciprocal_sqrt, bias=eps[:, 0:1], scale=1.0
+            )
+
+        def normalise_x(b, i):
+            if i == 0:
+                normed1[b] = work.tile([P, QUARTERS, C], F32, name="normed1")
+            nc.gpsimd.tensor_scalar(
+                out=normed1[b][:, i, :],
+                in0=x_tiles[b][:, i, :],
+                scalar1=neg_mean1[b][:, i : i + 1],
+                scalar2=rstd1[b][:, i : i + 1],
+                op0=ALU.add,
+                op1=ALU.mult,
+            )
+
+        def gain_bias_relu_x(b, t):
+            if t == 0:
+                y0T[b] = work.tile([P, PACK, BLOCK], BF16, name="y0T")
+            channels = psum.tile([P, BLOCK], F32, tag="channels")
+            for i in range(QUARTERS):
+                nc.tensor.transpose(
+                    channels[:, i * P : (i + 1) * P], normed1[b][:, i, t * P : (t + 1) * P], ident_f32[:]
                 )
-            std = small.tile([P, ROW_TILES], F32, name="std2")
-            nc.scalar.activation(out=std[:], in_=squares[:], func=ACT.Sqrt, bias=eps[:, 0:1], scale=1.0 / H)
-            rstd = small.tile([P, ROW_TILES], F32, name="rstd2")
-            nc.vector.reciprocal(out=rstd[:], in_=std[:])
-            for i in range(ROW_TILES):
-                nc.gpsimd.tensor_scalar(
-                    out=y1[:, i, :],
-                    in0=y1[:, i, :],
-                    scalar1=neg_mean[:, i : i + 1],
-                    scalar2=rstd[:, i : i + 1],
+            nc.scalar.activation(
+                out=y0T[b][:, t, :],
+                in_=channels[:],
+                func=ACT.Relu,
+                bias=params[:, PRE_B + t : PRE_B + t + 1],
+                scale=params[:, PRE_W + t : PRE_W + t + 1],
+            )
+
+        def group_y0(b):
+            grouped[b] = work.tile([P, BLOCK, PACK], BF16, name="grouped", align_bytes=64)
+            nc.vector.tensor_copy(
+                out=grouped[b][:].rearrange("p (n s) t -> p n t s", s=4),
+                in_=y0T[b][:].rearrange("p t (n s) -> p n t s", s=4),
+            )
+
+        def quantise_y0(b):
+            codes[b] = work.tile([P, BLOCK], U32, name="codes", align_bytes=64, bufs=3)
+            scales[b] = work.tile([P, BLOCK], U8, name="scales", align_bytes=64, bufs=3)
+            nc.vector.quantize_mx(
+                out=codes[b][:].bitcast(FP8X4),
+                scales=scales[b][:],
+                in_=grouped[b][:].rearrange("p n t -> p (n t)"),
+            )
+
+        def project(b, i):
+            if i == 0:
+                row_sums[b] = small.tile([P, QUARTERS, HALVES], F32, name="row_sums")
+            y1[b, i] = work.tile([P, H], F32, name="y1", bufs=LAG_FEATURES + QUARTERS - LAG_PROJECT + 1)
+            rows = slice(i * P, (i + 1) * P)
+            for half in range(HALVES):
+                cols = slice(half * BANK, (half + 1) * BANK)
+                acc = psum.tile([P, BANK], F32, tag="acc")
+                nc.tensor.matmul_mx(
+                    out=acc[:],
+                    lhsT=codes[b][:, rows].bitcast(FP8X4),
+                    lhsT_scale=scales[b][:, rows],
+                    rhs=w_codes[:, cols].bitcast(FP8X4),
+                    rhs_scale=w_scales[:, cols],
+                    start=True,
+                    stop=True,
+                )
+                nc.vector.scalar_tensor_tensor(
+                    out=y1[b, i][:, cols],
+                    in0=acc[:],
+                    scalar=0.0,
+                    in1=bias_all[:, cols],
                     op0=ALU.add,
-                    op1=ALU.mult,
+                    op1=ALU.add,
+                    accum_out=row_sums[b][:, i, half : half + 1],
                 )
-            return y1
 
-        def gain_bias_relu_store(b, normed):
-            resultT = work.tile([P, H_TILES, BLOCK], F32, name="resultT")
-            for j in range(H_TILES):
-                features = psum.tile([P, BLOCK], F32, tag="features")
-                for i in range(ROW_TILES):
-                    nc.tensor.transpose(
-                        features[:, i * P : (i + 1) * P], normed[:, i, j * P : (j + 1) * P], ident_f32[:]
-                    )
-                nc.scalar.activation(
-                    out=resultT[:, j, :],
-                    in_=features[:],
-                    func=ACT.Relu,
-                    bias=params[:, N1_B + j : N1_B + j + 1],
-                    scale=params[:, N1_W + j : N1_W + j + 1],
+        def mean_of_y1(b):
+            total = small.tile([P, QUARTERS], F32, name="total")
+            nc.vector.tensor_reduce(out=total[:], in_=row_sums[b][:], axis=AXIS.X, op=ALU.add)
+            neg_mean2[b] = small.tile([P, QUARTERS], F32, name="neg_mean2")
+            nc.vector.tensor_scalar_mul(out=neg_mean2[b][:], in0=total[:], scalar1=-1.0 / H)
+
+        def squares_of_y1(b, i):
+            if i == 0:
+                squares[b] = small.tile([P, QUARTERS], F32, name="squares")
+            unread = work.tile([P, H], BF16, name="unread")
+            nc.scalar.activation(
+                out=unread[:],
+                in_=y1[b, i][:],
+                func=ACT.Square,
+                bias=neg_mean2[b][:, i : i + 1],
+                scale=1.0,
+                accum_out=squares[b][:, i : i + 1],
+            )
+
+        def rstd_of_y1(b):
+            rstd2[b] = small.tile([P, QUARTERS], F32, name="rstd2")
+            nc.scalar.activation(
+                out=rstd2[b][:], in_=squares[b][:], func=ACT.Abs_reciprocal_sqrt, bias=eps[:, 0:1], scale=1.0 / H
+            )
+
+        def normalise_y1(b, i):
+            nc.gpsimd.tensor_scalar(
+                out=y1[b, i][:],
+                in0=y1[b, i][:],
+                scalar1=neg_mean2[b][:, i : i + 1],
+                scalar2=rstd2[b][:, i : i + 1],
+                op0=ALU.add,
+                op1=ALU.mult,
+            )
+
+        def gain_bias_relu_y1(b, j):
+            features = psum.tile([P, BLOCK], F32, tag="features")
+            for i in range(QUARTERS):
+                nc.tensor.transpose(features[:, i * P : (i + 1) * P], y1[b, i][:, j * P : (j + 1) * P], ident_f32[:])
+            resultT[b, j] = work.tile([P, BLOCK], F32, name="resultT", bufs=3 * TILES_PER_BANK)
+            nc.scalar.activation(
+                out=resultT[b, j][:],
+                in_=features[:],
+                func=ACT.Relu,
+                bias=params[:, N1_B + j : N1_B + j + 1],
+                scale=params[:, N1_W + j : N1_W + j + 1],
+            )
+
+        def turn_back_and_store(b, half, i):
+            back = psum.tile([P, BANK], F32, tag="back")
+            for q in range(TILES_PER_BANK):
+                nc.tensor.transpose(
+                    back[:, q * P : (q + 1) * P],
+                    resultT[b, half * TILES_PER_BANK + q][:, i * P : (i + 1) * P],
+                    ident_f32[:],
                 )
-            result = work.tile([P, ROW_TILES, H], F32, name="result")
-            for i in range(ROW_TILES):
-                for half in range(HALVES):
-                    back = psum.tile([P, BANK], F32, tag="back")
-                    for q in range(BANK // P):
-                        j = half * (BANK // P) + q
-                        nc.tensor.transpose(
-                            back[:, q * P : (q + 1) * P], resultT[:, j, i * P : (i + 1) * P], ident_f32[:]
-                        )
-                    if i == ROW_TILES - 1:
-                        nc.scalar.copy(out=result[:, i, half * BANK : (half + 1) * BANK], in_=back[:])
-                    else:
-                        nc.vector.tensor_copy(out=result[:, i, half * BANK : (half + 1) * BANK], in_=back[:])
-                nc.sync.dma_start(out=out_blocks[b][:, i, :], in_=result[:, i, :])
+            result = work.tile([P, BANK], F32, name="result", bufs=6)
+            nc.vector.tensor_copy(out=result[:], in_=back[:])
+            nc.sync.dma_start(out=out_blocks[b][:, i, half * BANK : (half + 1) * BANK], in_=result[:])
 
-        for b in range(BLOCKS):
-            codes, scales = first_norm(b)
-            normed = project_and_norm(b, codes, scales)
-            gain_bias_relu_store(b, normed)
+        for step in range(STEPS):
+            if 0 <= step - LAG_WEIGHTS < H_TILES:
+                turn_weights(step - LAG_WEIGHTS)
+            if step - LAG_WEIGHTS == H_TILES:
+                quantise_weights()
+
+            at = quarter_of(step, LAG_STATS)
+            if at is not None:
+                stats_of_x(at[0], at[1])
+            b = block_of(step, LAG_SCALARS1)
+            if b is not None:
+                scalars_of_x(b)
+            at = quarter_of(step, LAG_NORM1)
+            if at is not None:
+                normalise_x(at[0], at[1])
+            at = quarter_of(step, LAG_CHANNELS)
+            if at is not None:
+                gain_bias_relu_x(at[0], at[1])
+            b = block_of(step, LAG_QUANTISE)
+            if b is not None:
+                group_y0(b)
+            at = quarter_of(step, LAG_PROJECT)
+            if at is not None:
+                project(at[0], at[1])
+            if b is not None:
+                quantise_y0(b)
+            b = block_of(step, LAG_MEAN2)
+            if b is not None:
+                mean_of_y1(b)
+            at = quarter_of(step, LAG_SQUARES)
+            if at is not None:
+                squares_of_y1(at[0], at[1])
+            b = block_of(step, LAG_RSTD2)
+            if b is not None:
+                rstd_of_y1(b)
+            at = quarter_of(step, LAG_NORM2)
+            if at is not None:
+                normalise_y1(at[0], at[1])
+            at = quarter_of(step, LAG_FEATURES)
+            if at is not None:
+                for j in range(TILES_PER_STEP * at[1], TILES_PER_STEP * (at[1] + 1)):
+                    gain_bias_relu_y1(at[0], j)
+            at = quarter_of(step, LAG_BACK)
+            if at is not None:
+                for bank in range(TILES_PER_STEP * at[1], TILES_PER_STEP * (at[1] + 1)):
+                    turn_back_and_store(at[0], bank // QUARTERS, bank % QUARTERS)

@@ -10,7 +10,6 @@ U8 = mybir.dt.uint8
 FP8X4 = mybir.dt.float8_e4m3fn_x4
 ALU = mybir.AluOpType
 ACT = mybir.ActivationFunctionType
-AXIS = mybir.AxisListType
 
 P = 128
 PACK = 4
@@ -38,10 +37,8 @@ LAG_WEIGHTS = LAG_NORM1
 LAG_CHANNELS = LAG_NORM1 + QUARTERS
 LAG_QUANTISE = LAG_CHANNELS + QUARTERS
 LAG_PROJECT = LAG_QUANTISE + 1
-LAG_MEAN2 = LAG_PROJECT + QUARTERS - 1
-LAG_SQUARES = LAG_PROJECT + QUARTERS
-LAG_RSTD2 = LAG_SQUARES + QUARTERS - 1
-LAG_NORM2 = LAG_SQUARES + QUARTERS
+LAG_SQUARES = LAG_PROJECT + 1
+LAG_NORM2 = LAG_SQUARES + 1
 LAG_FEATURES = LAG_NORM2 + QUARTERS
 LAG_BACK = LAG_FEATURES + QUARTERS // HALVES
 STEPS = LAG_BACK + BLOCKS * QUARTERS
@@ -211,11 +208,17 @@ def tile_graphresblock_pa_t_kernel(tc, x, pre_w, pre_b, lin1_W, lin1_b, n1_w, n1
                     accum_out=row_sums[b][:, i, half : half + 1],
                 )
 
-        def mean_of_y1(b):
-            total = small.tile([P, QUARTERS], F32, name="total")
-            nc.vector.tensor_reduce(out=total[:], in_=row_sums[b][:], axis=AXIS.X, op=ALU.add)
-            neg_mean2[b] = small.tile([P, QUARTERS], F32, name="neg_mean2")
-            nc.vector.tensor_scalar_mul(out=neg_mean2[b][:], in0=total[:], scalar1=-1.0 / H)
+        def mean_of_y1(b, i):
+            if i == 0:
+                neg_mean2[b] = small.tile([P, QUARTERS], F32, name="neg_mean2")
+            nc.vector.tensor_scalar(
+                out=neg_mean2[b][:, i : i + 1],
+                in0=row_sums[b][:, i, 0:1],
+                scalar1=row_sums[b][:, i, 1:2],
+                scalar2=-1.0 / H,
+                op0=ALU.add,
+                op1=ALU.mult,
+            )
 
         def squares_of_y1(b, i):
             if i == 0:
@@ -230,10 +233,15 @@ def tile_graphresblock_pa_t_kernel(tc, x, pre_w, pre_b, lin1_W, lin1_b, n1_w, n1
                 accum_out=squares[b][:, i : i + 1],
             )
 
-        def rstd_of_y1(b):
-            rstd2[b] = small.tile([P, QUARTERS], F32, name="rstd2")
+        def rstd_of_y1(b, i):
+            if i == 0:
+                rstd2[b] = small.tile([P, QUARTERS], F32, name="rstd2")
             nc.scalar.activation(
-                out=rstd2[b][:], in_=squares[b][:], func=ACT.Abs_reciprocal_sqrt, bias=eps[:, 0:1], scale=1.0 / H
+                out=rstd2[b][:, i : i + 1],
+                in_=squares[b][:, i : i + 1],
+                func=ACT.Abs_reciprocal_sqrt,
+                bias=eps[:, 0:1],
+                scale=1.0 / H,
             )
 
         def normalise_y1(b, i):
@@ -297,15 +305,9 @@ def tile_graphresblock_pa_t_kernel(tc, x, pre_w, pre_b, lin1_W, lin1_b, n1_w, n1
                 project(at[0], at[1])
             if b is not None:
                 quantise_y0(b)
-            b = block_of(step, LAG_MEAN2)
-            if b is not None:
-                mean_of_y1(b)
             at = quarter_of(step, LAG_SQUARES)
             if at is not None:
                 squares_of_y1(at[0], at[1])
-            b = block_of(step, LAG_RSTD2)
-            if b is not None:
-                rstd_of_y1(b)
             at = quarter_of(step, LAG_NORM2)
             if at is not None:
                 normalise_y1(at[0], at[1])
@@ -317,3 +319,9 @@ def tile_graphresblock_pa_t_kernel(tc, x, pre_w, pre_b, lin1_W, lin1_b, n1_w, n1
             if at is not None:
                 for bank in range(TILES_PER_STEP * at[1], TILES_PER_STEP * (at[1] + 1)):
                     turn_back_and_store(at[0], bank // QUARTERS, bank % QUARTERS)
+            at = quarter_of(step, LAG_PROJECT)
+            if at is not None:
+                mean_of_y1(at[0], at[1])
+            at = quarter_of(step, LAG_SQUARES)
+            if at is not None:
+                rstd_of_y1(at[0], at[1])

@@ -31,10 +31,9 @@ PRE_W, PRE_B, N1_W, N1_B = 0, PACK, 2 * PACK, 2 * PACK + H_TILES
 PARAM_COLS = 2 * PACK + 2 * H_TILES
 
 LAG_STATS = 0
-LAG_SCALARS1 = LAG_STATS + QUARTERS - 1
-LAG_NORM1 = LAG_STATS + QUARTERS
-LAG_WEIGHTS = LAG_NORM1
+LAG_NORM1 = LAG_STATS + 1
 LAG_CHANNELS = LAG_NORM1 + QUARTERS
+LAG_WEIGHTS = LAG_CHANNELS
 LAG_QUANTISE = LAG_CHANNELS + QUARTERS
 LAG_PROJECT = LAG_QUANTISE + 1
 LAG_SQUARES = LAG_PROJECT + 1
@@ -118,7 +117,7 @@ def tile_graphresblock_pa_t_kernel(tc, x, pre_w, pre_b, lin1_W, lin1_b, n1_w, n1
                 in_=w_grouped[:].rearrange("p h t -> p (h t)"),
             )
 
-        stats, neg_mean1, rstd1, normed1, y0T, grouped, codes, scales = {}, {}, {}, {}, {}, {}, {}, {}
+        stats, mean_var, neg_mean1, rstd1, normed1, y0T, grouped, codes, scales = {}, {}, {}, {}, {}, {}, {}, {}, {}
         y1, row_sums, neg_mean2, squares, rstd2, resultT = {}, {}, {}, {}, {}, {}
 
         def stats_of_x(b, i):
@@ -126,20 +125,24 @@ def tile_graphresblock_pa_t_kernel(tc, x, pre_w, pre_b, lin1_W, lin1_b, n1_w, n1
                 stats[b] = small.tile([P, QUARTERS, BN_STATS_DIM], F32, name="stats")
             nc.vector.bn_stats(out=stats[b][:, i, :], in_=x_tiles[b][:, i, :])
 
-        def scalars_of_x(b):
-            mean_var = small.tile([P, QUARTERS, BN_AGGR_DIM], F32, name="mean_var")
-            for i in range(QUARTERS):
-                nc.vector.bn_aggr(out=mean_var[:, i, :], in_=stats[b][:, i, :])
-            neg_mean1[b] = small.tile([P, QUARTERS], F32, name="neg_mean1")
-            nc.vector.tensor_scalar_mul(out=neg_mean1[b][:], in0=mean_var[:, :, 0], scalar1=-1.0)
-            rstd1[b] = small.tile([P, QUARTERS], F32, name="rstd1")
-            nc.scalar.activation(
-                out=rstd1[b][:], in_=mean_var[:, :, 1], func=ACT.Abs_reciprocal_sqrt, bias=eps[:, 0:1], scale=1.0
-            )
+        def mean_of_x(b, i):
+            if i == 0:
+                mean_var[b] = small.tile([P, QUARTERS, BN_AGGR_DIM], F32, name="mean_var")
+                neg_mean1[b] = small.tile([P, QUARTERS], F32, name="neg_mean1")
+            nc.vector.bn_aggr(out=mean_var[b][:, i, :], in_=stats[b][:, i, :])
+            nc.vector.tensor_scalar_mul(out=neg_mean1[b][:, i : i + 1], in0=mean_var[b][:, i, 0:1], scalar1=-1.0)
 
         def normalise_x(b, i):
             if i == 0:
+                rstd1[b] = small.tile([P, QUARTERS], F32, name="rstd1")
                 normed1[b] = work.tile([P, QUARTERS, C], F32, name="normed1")
+            nc.scalar.activation(
+                out=rstd1[b][:, i : i + 1],
+                in_=mean_var[b][:, i, 1:2],
+                func=ACT.Abs_reciprocal_sqrt,
+                bias=eps[:, 0:1],
+                scale=1.0,
+            )
             nc.gpsimd.tensor_scalar(
                 out=normed1[b][:, i, :],
                 in0=x_tiles[b][:, i, :],
@@ -280,17 +283,15 @@ def tile_graphresblock_pa_t_kernel(tc, x, pre_w, pre_b, lin1_W, lin1_b, n1_w, n1
             nc.sync.dma_start(out=out_blocks[b][:, i, half * BANK : (half + 1) * BANK], in_=result[:])
 
         for step in range(STEPS):
-            if 0 <= step - LAG_WEIGHTS < H_TILES:
-                turn_weights(step - LAG_WEIGHTS)
-            if step - LAG_WEIGHTS == H_TILES:
+            if 0 <= step - LAG_WEIGHTS < QUARTERS:
+                for j in range(TILES_PER_STEP * (step - LAG_WEIGHTS), TILES_PER_STEP * (step - LAG_WEIGHTS + 1)):
+                    turn_weights(j)
+            if step - LAG_WEIGHTS == QUARTERS:
                 quantise_weights()
 
             at = quarter_of(step, LAG_STATS)
             if at is not None:
                 stats_of_x(at[0], at[1])
-            b = block_of(step, LAG_SCALARS1)
-            if b is not None:
-                scalars_of_x(b)
             at = quarter_of(step, LAG_NORM1)
             if at is not None:
                 normalise_x(at[0], at[1])
@@ -319,6 +320,9 @@ def tile_graphresblock_pa_t_kernel(tc, x, pre_w, pre_b, lin1_W, lin1_b, n1_w, n1
             if at is not None:
                 for bank in range(TILES_PER_STEP * at[1], TILES_PER_STEP * (at[1] + 1)):
                     turn_back_and_store(at[0], bank // QUARTERS, bank % QUARTERS)
+            at = quarter_of(step, LAG_STATS)
+            if at is not None:
+                mean_of_x(at[0], at[1])
             at = quarter_of(step, LAG_PROJECT)
             if at is not None:
                 mean_of_y1(at[0], at[1])

@@ -31,9 +31,10 @@ PRE_W, PRE_B, N1_W, N1_B = 0, PACK, 2 * PACK, 2 * PACK + H_TILES
 PARAM_COLS = 2 * PACK + 2 * H_TILES
 
 LAG_STATS = 0
-LAG_NORM1 = LAG_STATS + 1
+LAG_SCALARS1 = LAG_STATS + QUARTERS - 1
+LAG_NORM1 = LAG_STATS + QUARTERS
+LAG_WEIGHTS = LAG_NORM1
 LAG_CHANNELS = LAG_NORM1 + QUARTERS
-LAG_WEIGHTS = LAG_CHANNELS
 LAG_QUANTISE = LAG_CHANNELS + QUARTERS
 LAG_PROJECT = LAG_QUANTISE + 1
 LAG_SQUARES = LAG_PROJECT + 1
@@ -117,7 +118,7 @@ def tile_graphresblock_pa_t_kernel(tc, x, pre_w, pre_b, lin1_W, lin1_b, n1_w, n1
                 in_=w_grouped[:].rearrange("p h t -> p (h t)"),
             )
 
-        stats, mean_var, neg_mean1, rstd1, normed1, y0T, grouped, codes, scales = {}, {}, {}, {}, {}, {}, {}, {}, {}
+        stats, neg_mean1, rstd1, normed1, y0T, grouped, codes, scales = {}, {}, {}, {}, {}, {}, {}, {}
         y1, row_sums, neg_mean2, squares, rstd2, resultT = {}, {}, {}, {}, {}, {}
 
         def stats_of_x(b, i):
@@ -125,24 +126,20 @@ def tile_graphresblock_pa_t_kernel(tc, x, pre_w, pre_b, lin1_W, lin1_b, n1_w, n1
                 stats[b] = small.tile([P, QUARTERS, BN_STATS_DIM], F32, name="stats")
             nc.vector.bn_stats(out=stats[b][:, i, :], in_=x_tiles[b][:, i, :])
 
-        def mean_of_x(b, i):
-            if i == 0:
-                mean_var[b] = small.tile([P, QUARTERS, BN_AGGR_DIM], F32, name="mean_var")
-                neg_mean1[b] = small.tile([P, QUARTERS], F32, name="neg_mean1")
-            nc.vector.bn_aggr(out=mean_var[b][:, i, :], in_=stats[b][:, i, :])
-            nc.vector.tensor_scalar_mul(out=neg_mean1[b][:, i : i + 1], in0=mean_var[b][:, i, 0:1], scalar1=-1.0)
+        def scalars_of_x(b):
+            mean_var = small.tile([P, QUARTERS, BN_AGGR_DIM], F32, name="mean_var")
+            for i in range(QUARTERS):
+                nc.vector.bn_aggr(out=mean_var[:, i, :], in_=stats[b][:, i, :])
+            neg_mean1[b] = small.tile([P, QUARTERS], F32, name="neg_mean1")
+            nc.vector.tensor_scalar_mul(out=neg_mean1[b][:], in0=mean_var[:, :, 0], scalar1=-1.0)
+            rstd1[b] = small.tile([P, QUARTERS], F32, name="rstd1")
+            nc.scalar.activation(
+                out=rstd1[b][:], in_=mean_var[:, :, 1], func=ACT.Abs_reciprocal_sqrt, bias=eps[:, 0:1], scale=1.0
+            )
 
         def normalise_x(b, i):
             if i == 0:
-                rstd1[b] = small.tile([P, QUARTERS], F32, name="rstd1")
                 normed1[b] = work.tile([P, QUARTERS, C], F32, name="normed1")
-            nc.scalar.activation(
-                out=rstd1[b][:, i : i + 1],
-                in_=mean_var[b][:, i, 1:2],
-                func=ACT.Abs_reciprocal_sqrt,
-                bias=eps[:, 0:1],
-                scale=1.0,
-            )
             nc.gpsimd.tensor_scalar(
                 out=normed1[b][:, i, :],
                 in0=x_tiles[b][:, i, :],
@@ -279,19 +276,24 @@ def tile_graphresblock_pa_t_kernel(tc, x, pre_w, pre_b, lin1_W, lin1_b, n1_w, n1
                     ident_f32[:],
                 )
             result = work.tile([P, BANK], F32, name="result", bufs=6)
-            nc.vector.tensor_copy(out=result[:], in_=back[:])
+            if i == QUARTERS - 1:
+                nc.scalar.copy(out=result[:], in_=back[:])
+            else:
+                nc.vector.tensor_copy(out=result[:], in_=back[:])
             nc.sync.dma_start(out=out_blocks[b][:, i, half * BANK : (half + 1) * BANK], in_=result[:])
 
         for step in range(STEPS):
-            if 0 <= step - LAG_WEIGHTS < QUARTERS:
-                for j in range(TILES_PER_STEP * (step - LAG_WEIGHTS), TILES_PER_STEP * (step - LAG_WEIGHTS + 1)):
-                    turn_weights(j)
-            if step - LAG_WEIGHTS == QUARTERS:
+            if 0 <= step - LAG_WEIGHTS < H_TILES:
+                turn_weights(step - LAG_WEIGHTS)
+            if step - LAG_WEIGHTS == H_TILES:
                 quantise_weights()
 
             at = quarter_of(step, LAG_STATS)
             if at is not None:
                 stats_of_x(at[0], at[1])
+            b = block_of(step, LAG_SCALARS1)
+            if b is not None:
+                scalars_of_x(b)
             at = quarter_of(step, LAG_NORM1)
             if at is not None:
                 normalise_x(at[0], at[1])
@@ -320,9 +322,6 @@ def tile_graphresblock_pa_t_kernel(tc, x, pre_w, pre_b, lin1_W, lin1_b, n1_w, n1
             if at is not None:
                 for bank in range(TILES_PER_STEP * at[1], TILES_PER_STEP * (at[1] + 1)):
                     turn_back_and_store(at[0], bank // QUARTERS, bank % QUARTERS)
-            at = quarter_of(step, LAG_STATS)
-            if at is not None:
-                mean_of_x(at[0], at[1])
             at = quarter_of(step, LAG_PROJECT)
             if at is not None:
                 mean_of_y1(at[0], at[1])

from contextlib import ExitStack

import concourse.mybir as mybir
from concourse.masks import make_identity

F32 = mybir.dt.float32
BF16 = mybir.dt.bfloat16
U32 = mybir.dt.uint32
U8 = mybir.dt.uint8
FP8X4 = mybir.dt.float8_e4m3fn_x4
ALU = mybir.AluOpType
ACT = mybir.ActivationFunctionType

P = 128
PACK = 4
ROWS = 4 * 1024
C = 512
H = 1024
EPS = 1e-12
QUARTERS = 4
BLOCK = QUARTERS * P
BLOCKS = ROWS // BLOCK
BANK = 512
HALVES = H // BANK
H_TILES = H // P
TILES_PER_BANK = BANK // P
TILES_PER_STEP = H_TILES // QUARTERS
BN_STATS_DIM = 6
BN_AGGR_DIM = 2
PRE_W, PRE_B, N1_W, N1_B = 0, PACK, 2 * PACK, 2 * PACK + H_TILES
PARAM_COLS = 2 * PACK + 2 * H_TILES

LAG_STATS = 0
LAG_SCALARS1 = LAG_STATS + QUARTERS - 1
LAG_NORM1 = LAG_STATS + QUARTERS
LAG_WEIGHTS = LAG_NORM1
LAG_CHANNELS = LAG_NORM1 + QUARTERS
LAG_QUANTISE = LAG_CHANNELS + QUARTERS
LAG_PROJECT = LAG_QUANTISE + 1
LAG_SQUARES = LAG_PROJECT + 1
LAG_NORM2 = LAG_SQUARES + 1
LAG_FEATURES = LAG_NORM2 + QUARTERS
LAG_BACK = LAG_FEATURES + QUARTERS // HALVES
STEPS = LAG_BACK + BLOCKS * QUARTERS

FLOPS = 2 * ROWS * C * H


def quarter_of(step, lag):
    index = step - lag
    if 0 <= index < BLOCKS * QUARTERS:
        return divmod(index, QUARTERS)
    return None


def block_of(step, lag):
    index = step - lag
    if index >= 0 and index % QUARTERS == 0 and index // QUARTERS < BLOCKS:
        return index // QUARTERS
    return None


def tile_graphresblock_pa_t_kernel(tc, x, pre_w, pre_b, lin1_W, lin1_b, n1_w, n1_b, out):
    nc = tc.nc
    x_blocks = x.flatten_outer_dims().rearrange("(b p i) c -> b p i c", p=P, i=QUARTERS)
    out_blocks = out.flatten_outer_dims().rearrange("(b p i) h -> b p i h", p=P, i=QUARTERS)

    with ExitStack() as ctx:
        ctx.enter_context(tc.manual_schedule())
        keep = ctx.enter_context(tc.tile_pool(name="keep", bufs=1))
        small = ctx.enter_context(tc.tile_pool(name="small", bufs=4))
        work = ctx.enter_context(tc.tile_pool(name="work", bufs=2))
        psum = ctx.enter_context(tc.psum_pool(name="psum", bufs=2))

        eps = keep.tile([P, 1], F32)
        nc.vector.memset(eps[:], EPS)
        table_warmer = keep.tile([P, 1], F32)
        nc.scalar.activation(out=table_warmer[:], in_=eps[:], func=ACT.Abs_reciprocal_sqrt)
        param_rows = keep.tile([P, P], BF16)
        nc.vector.memset(param_rows[:], 0.0)
        ident_bf16 = keep.tile([P, P], BF16)
        make_identity(nc, ident_bf16[:])
        ident_f32 = keep.tile([P, P], F32)
        make_identity(nc, ident_f32[:])

        x_tiles = [keep.tile([P, QUARTERS, C], BF16, name="x%d" % b) for b in range(BLOCKS)]
        w_rows = keep.tile([P, H_TILES, C], BF16)
        bias_all = keep.tile([P, H], BF16)
        nc.sync.dma_start(out=x_tiles[0][:], in_=x_blocks[0])
        for first, vector in ((PRE_W, pre_w), (PRE_B, pre_b), (N1_W, n1_w), (N1_B, n1_b)):
            rows = vector.rearrange("(t p) -> t p", p=P)
            nc.sync.dma_start(out=param_rows[first : first + rows.shape[0], :], in_=rows)
        nc.sync.dma_start(out=x_tiles[1][:], in_=x_blocks[1])
        nc.sync.dma_start(out=w_rows[:], in_=lin1_W.rearrange("(j p) c -> p j c", p=P))
        for b in range(2, BLOCKS):
            nc.sync.dma_start(out=x_tiles[b][:], in_=x_blocks[b])
        nc.sync.dma_start(out=bias_all[:], in_=lin1_b.partition_broadcast(P))

        params_ps = psum.tile([P, P], BF16, tag="channels")
        nc.tensor.transpose(params_ps[:], param_rows[:], ident_bf16[:])
        params = keep.tile([P, PARAM_COLS], F32)
        nc.scalar.copy(out=params[:], in_=params_ps[:, 0:PARAM_COLS])

        w_grouped = keep.tile([P, H, PACK], BF16, align_bytes=64)
        w_codes = keep.tile([P, H], U32, align_bytes=64)
        w_scales = keep.tile([P, H], U8, align_bytes=64)

        def turn_weights(j):
            w_ps = psum.tile([P, PACK, P], BF16, tag="channels")
            for t in range(PACK):
                nc.tensor.transpose(w_ps[:, t, :], w_rows[:, j, t * P : (t + 1) * P], ident_bf16[:])
            nc.scalar.copy(out=w_grouped[:, j * P : (j + 1) * P, :], in_=w_ps[:].rearrange("p t h -> p h t"))

        def quantise_weights():
            nc.vector.quantize_mx(
                out=w_codes[:].bitcast(FP8X4),
                scales=w_scales[:],
                in_=w_grouped[:].rearrange("p h t -> p (h t)"),
            )

        stats, neg_mean1, rstd1, normed1, y0T, grouped, codes, scales = {}, {}, {}, {}, {}, {}, {}, {}
        y1, row_sums, neg_mean2, squares, rstd2, resultT = {}, {}, {}, {}, {}, {}

        def stats_of_x(b, i):
            if i == 0:
                stats[b] = small.tile([P, QUARTERS, BN_STATS_DIM], F32, name="stats")
            nc.vector.bn_stats(out=stats[b][:, i, :], in_=x_tiles[b][:, i, :])

        def scalars_of_x(b):
            mean_var = small.tile([P, QUARTERS, BN_AGGR_DIM], F32, name="mean_var")
            for i in range(QUARTERS):
                nc.vector.bn_aggr(out=mean_var[:, i, :], in_=stats[b][:, i, :])
            neg_mean1[b] = small.tile([P, QUARTERS], F32, name="neg_mean1")
            nc.vector.tensor_scalar_mul(out=neg_mean1[b][:], in0=mean_var[:, :, 0], scalar1=-1.0)
            rstd1[b] = small.tile([P, QUARTERS], F32, name="rstd1")
            nc.scalar.activation(
                out=rstd1[b][:], in_=mean_var[:, :, 1], func=ACT.Abs_reciprocal_sqrt, bias=eps[:, 0:1], scale=1.0
            )

        def normalise_x(b, i):
            if i == 0:
                normed1[b] = work.tile([P, QUARTERS, C], F32, name="normed1")
            nc.gpsimd.tensor_scalar(
                out=normed1[b][:, i, :],
                in0=x_tiles[b][:, i, :],
                scalar1=neg_mean1[b][:, i : i + 1],
                scalar2=rstd1[b][:, i : i + 1],
                op0=ALU.add,
                op1=ALU.mult,
            )

        def gain_bias_relu_x(b, t):
            if t == 0:
                y0T[b] = work.tile([P, PACK, BLOCK], BF16, name="y0T")
            channels = psum.tile([P, BLOCK], F32, tag="channels")
            for i in range(QUARTERS):
                nc.tensor.transpose(
                    channels[:, i * P : (i + 1) * P], normed1[b][:, i, t * P : (t + 1) * P], ident_f32[:]
                )
            nc.scalar.activation(
                out=y0T[b][:, t, :],
                in_=channels[:],
                func=ACT.Relu,
                bias=params[:, PRE_B + t : PRE_B + t + 1],
                scale=params[:, PRE_W + t : PRE_W + t + 1],
            )

        def group_y0(b):
            grouped[b] = work.tile([P, BLOCK, PACK], BF16, name="grouped", align_bytes=64)
            nc.vector.tensor_copy(
                out=grouped[b][:].rearrange("p (n s) t -> p n t s", s=4),
                in_=y0T[b][:].rearrange("p t (n s) -> p n t s", s=4),
            )

        def quantise_y0(b):
            codes[b] = work.tile([P, BLOCK], U32, name="codes", align_bytes=64, bufs=3)
            scales[b] = work.tile([P, BLOCK], U8, name="scales", align_bytes=64, bufs=3)
            nc.vector.quantize_mx(
                out=codes[b][:].bitcast(FP8X4),
                scales=scales[b][:],
                in_=grouped[b][:].rearrange("p n t -> p (n t)"),
            )

        def project(b, i):
            if i == 0:
                row_sums[b] = small.tile([P, QUARTERS, HALVES], F32, name="row_sums")
            y1[b, i] = work.tile([P, H], F32, name="y1", bufs=LAG_FEATURES + QUARTERS - LAG_PROJECT + 1)
            rows = slice(i * P, (i + 1) * P)
            for half in range(HALVES):
                cols = slice(half * BANK, (half + 1) * BANK)
                acc = psum.tile([P, BANK], F32, tag="acc")
                nc.tensor.matmul_mx(
                    out=acc[:],
                    lhsT=codes[b][:, rows].bitcast(FP8X4),
                    lhsT_scale=scales[b][:, rows],
                    rhs=w_codes[:, cols].bitcast(FP8X4),
                    rhs_scale=w_scales[:, cols],
                    start=True,
                    stop=True,
                )
                nc.vector.scalar_tensor_tensor(
                    out=y1[b, i][:, cols],
                    in0=acc[:],
                    scalar=0.0,
                    in1=bias_all[:, cols],
                    op0=ALU.add,
                    op1=ALU.add,
                    accum_out=row_sums[b][:, i, half : half + 1],
                )

        def mean_of_y1(b, i):
            if i == 0:
                neg_mean2[b] = small.tile([P, QUARTERS], F32, name="neg_mean2")
            nc.vector.tensor_scalar(
                out=neg_mean2[b][:, i : i + 1],
                in0=row_sums[b][:, i, 0:1],
                scalar1=row_sums[b][:, i, 1:2],
                scalar2=-1.0 / H,
                op0=ALU.add,
                op1=ALU.mult,
            )

        def squares_of_y1(b, i):
            if i == 0:
                squares[b] = small.tile([P, QUARTERS], F32, name="squares")
            unread = work.tile([P, H], BF16, name="unread")
            nc.scalar.activation(
                out=unread[:],
                in_=y1[b, i][:],
                func=ACT.Square,
                bias=neg_mean2[b][:, i : i + 1],
                scale=1.0,
                accum_out=squares[b][:, i : i + 1],
            )

        def rstd_of_y1(b, i):
            if i == 0:
                rstd2[b] = small.tile([P, QUARTERS], F32, name="rstd2")
            nc.scalar.activation(
                out=rstd2[b][:, i : i + 1],
                in_=squares[b][:, i : i + 1],
                func=ACT.Abs_reciprocal_sqrt,
                bias=eps[:, 0:1],
                scale=1.0 / H,
            )

        def normalise_y1(b, i):
            nc.gpsimd.tensor_scalar(
                out=y1[b, i][:],
                in0=y1[b, i][:],
                scalar1=neg_mean2[b][:, i : i + 1],
                scalar2=rstd2[b][:, i : i + 1],
                op0=ALU.add,
                op1=ALU.mult,
            )

        def gain_bias_relu_y1(b, j):
            features = psum.tile([P, BLOCK], F32, tag="features")
            for i in range(QUARTERS):
                nc.tensor.transpose(features[:, i * P : (i + 1) * P], y1[b, i][:, j * P : (j + 1) * P], ident_f32[:])
            resultT[b, j] = work.tile([P, BLOCK], F32, name="resultT", bufs=3 * TILES_PER_BANK)
            nc.scalar.activation(
                out=resultT[b, j][:],
                in_=features[:],
                func=ACT.Relu,
                bias=params[:, N1_B + j : N1_B + j + 1],
                scale=params[:, N1_W + j : N1_W + j + 1],
            )

        def turn_back_and_store(b, half, i):
            back = psum.tile([P, BANK], F32, tag="back")
            for q in range(TILES_PER_BANK):
                nc.tensor.transpose(
                    back[:, q * P : (q + 1) * P],
                    resultT[b, half * TILES_PER_BANK + q][:, i * P : (i + 1) * P],
                    ident_f32[:],
                )
            result = work.tile([P, BANK], F32, name="result", bufs=6)
            if i == QUARTERS - 1:
                nc.scalar.copy(out=result[:], in_=back[:])
            else:
                nc.vector.tensor_copy(out=result[:], in_=back[:])
            nc.sync.dma_start(out=out_blocks[b][:, i, half * BANK : (half + 1) * BANK], in_=result[:])

        for step in range(STEPS):
            if 0 <= step - LAG_WEIGHTS < H_TILES:
                turn_weights(step - LAG_WEIGHTS)
            if step - LAG_WEIGHTS == H_TILES:
                quantise_weights()

            at = quarter_of(step, LAG_STATS)
            if at is not None:
                stats_of_x(at[0], at[1])
            b = block_of(step, LAG_SCALARS1)
            if b is not None:
                scalars_of_x(b)
            at = quarter_of(step, LAG_NORM1)
            if at is not None:
                normalise_x(at[0], at[1])
            at = quarter_of(step, LAG_CHANNELS)
            if at is not None:
                gain_bias_relu_x(at[0], at[1])
            b = block_of(step, LAG_QUANTISE)
            if b is not None:
                group_y0(b)
            at = quarter_of(step, LAG_PROJECT)
            if at is not None:
                project(at[0], at[1])
            if b is not None:
                quantise_y0(b)
            at = quarter_of(step, LAG_SQUARES)
            if at is not None:
                squares_of_y1(at[0], at[1])
            at = quarter_of(step, LAG_NORM2)
            if at is not None:
                normalise_y1(at[0], at[1])
            at = quarter_of(step, LAG_FEATURES)
            if at is not None:
                for j in range(TILES_PER_STEP * at[1], TILES_PER_STEP * (at[1] + 1)):
                    gain_bias_relu_y1(at[0], j)
            at = quarter_of(step, LAG_BACK)
            if at is not None:
                for bank in range(TILES_PER_STEP * at[1], TILES_PER_STEP * (at[1] + 1)):
                    turn_back_and_store(at[0], bank // QUARTERS, bank % QUARTERS)
            at = quarter_of(step, LAG_PROJECT)
            if at is not None:
                mean_of_y1(at[0], at[1])
            at = quarter_of(step, LAG_SQUARES)
            if at is not None:
                rstd_of_y1(at[0], at[1])
